import numpy as np
import ml_dtypes


def mxq(x, axis, fmt="e4m3"):
    dtype, down = {"e4m3": (ml_dtypes.float8_e4m3fn, 7), "e5m2": (ml_dtypes.float8_e5m2, 14)}[fmt]
    v = np.moveaxis(np.asarray(x, np.float32).astype(ml_dtypes.bfloat16).astype(np.float64), axis, -1)
    blocks = v.reshape(v.shape[:-1] + (-1, 32))
    amax = np.abs(blocks).max(-1, keepdims=True)
    byte = np.maximum(np.where(amax > 0, np.frexp(amax)[1] - 1 + 127, 0) - down, 1)
    scale = np.exp2(byte - 127.0)
    codes = (blocks / scale).astype(np.float32).astype(dtype).astype(np.float64)
    return np.moveaxis((codes * scale).reshape(v.shape), -1, axis)


WIDE = False


def mx_kscale(k):
    if not WIDE:
        return np.ones(k)
    levels = np.array([20, -20, 10, -10, 0])
    a = np.random.permutation(np.resize(levels, k // 512 * 4)).reshape(k // 512, 4)
    idx = np.arange(k)
    return np.exp2(a[idx // 512, idx % 128 // 32])


BF16 = ml_dtypes.bfloat16


def bf(x):
    return np.asarray(x, np.float32).astype(BF16)


def f64(x):
    return np.asarray(x).astype(np.float64)


B, C, H, W, F, KH, KW = 8, 512, 32, 32, 512, 1, 1
OW, OH = W - KW + 1, H - KH + 1
K = KH * KW * C
SPARSITY = 0.7


def setup_inputs():
    u = mx_kscale(F)
    limit = np.sqrt(6.0 / (F + K))
    vals = np.random.uniform(-limit, limit, (F, K))
    mask = np.random.random((F, K)) >= SPARSITY
    mask[::32, :] = True
    x = np.random.standard_normal((B, C, H, W))
    g = np.random.standard_normal((B, F, OW, OH)) * np.exp2(np.random.randint(-12, 1, (B, 1, OW, OH))) * 8.0
    return {"inputs": bf(x),
            "kernel": bf(vals * mask / u[:, None]),
            "grad_out": bf(g * u[None, :, None, None])}


def reference(inputs, kernel, grad_out):
    g = np.transpose(f64(grad_out), (0, 2, 3, 1))
    g2 = np.ascontiguousarray(g.reshape(-1, F))
    gp = mxq(g2, 1, "e5m2") @ mxq(f64(kernel), 0, "e4m3")
    gx = gp.reshape(B, OW, OH, C)
    return np.ascontiguousarray(np.transpose(gx, (0, 3, 2, 1)))

@@ -1,0 +1,100 @@
+from contextlib import ExitStack
+
+import concourse.mybir as mybir
+
+BF16 = mybir.dt.bfloat16
+F32 = mybir.dt.float32
+U32 = mybir.dt.uint32
+U8 = mybir.dt.uint8
+E4M3_X4 = mybir.dt.float8_e4m3fn_x4
+E5M2_X4 = mybir.dt.float8_e5m2_x4
+
+P = 128
+PACK = 4
+
+BATCH = 8
+FEATURES = 512
+CHANNELS = 512
+SIDE = 32
+TOKENS = SIDE * SIDE
+
+assert FEATURES == P * PACK
+
+GROUPS = CHANNELS // P
+PASS_TOKENS = 512
+PASS_A = PASS_TOKENS // SIDE
+PASSES = TOKENS // PASS_TOKENS
+PSUM_BANKS = 8
+RUN = 4
+
+FLOPS = 2 * BATCH * TOKENS * FEATURES * CHANNELS
+BYTES = 2 * BATCH * FEATURES * TOKENS + 2 * FEATURES * CHANNELS + 4 * BATCH * CHANNELS * TOKENS
+
+
+def tile_sparseconv2d_t_kernel(tc, inputs, kernel, grad_out, out):
+    nc = tc.nc
+    with ExitStack() as ctx:
+        weights = ctx.enter_context(tc.tile_pool(name="weights", bufs=1))
+        loaded = ctx.enter_context(tc.tile_pool(name="loaded", bufs=BATCH))
+        results = ctx.enter_context(tc.tile_pool(name="results", bufs=BATCH))
+        stage = ctx.enter_context(tc.tile_pool(name="stage", bufs=3))
+        banks = ctx.enter_context(tc.psum_pool(name="banks", bufs=PSUM_BANKS))
+
+        k_rows = weights.tile([P, PACK, CHANNELS], BF16)
+        nc.sync.dma_start(out=k_rows[:], in_=kernel.rearrange("(p j) c -> p j c", j=PACK))
+        g_rows = []
+        for b in range(BATCH):
+            rows = loaded.tile([P, PACK, TOKENS], BF16, name="rows")
+            nc.sync.dma_start(
+                out=rows[:], in_=grad_out[b].rearrange("(p j) a d -> p j (a d)", j=PACK)
+            )
+            g_rows.append(rows)
+
+        k_grouped = weights.tile([P, GROUPS, P, PACK], BF16, align_bytes=64)
+        nc.vector.tensor_copy(
+            out=k_grouped[:], in_=k_rows[:].rearrange("p j (m i) -> p i m j", i=GROUPS)
+        )
+        k_codes = weights.tile([P, GROUPS * P], U32, align_bytes=64)
+        k_scales = weights.tile([P, GROUPS * P], U8, align_bytes=64)
+        nc.vector.quantize_mx(
+            out=k_codes[:].bitcast(E4M3_X4),
+            scales=k_scales[:],
+            in_=k_grouped[:].rearrange("p i m j -> p (i m j)"),
+        )
+
+        for b in range(BATCH):
+            result = results.tile([P, GROUPS, SIDE, SIDE], F32)
+            for t in range(PASSES):
+                tokens = slice(t * PASS_TOKENS, (t + 1) * PASS_TOKENS)
+                g_grouped = stage.tile([P, PASS_TOKENS, PACK], BF16, align_bytes=64)
+                nc.vector.tensor_copy(
+                    out=g_grouped[:].rearrange("p (n r) j -> p n j r", r=RUN),
+                    in_=g_rows[b][:, :, tokens].rearrange("p j (n r) -> p n j r", r=RUN),
+                )
+                g_codes = stage.tile([P, PASS_TOKENS], U32, align_bytes=64)
+                g_scales = stage.tile([P, PASS_TOKENS], U8, align_bytes=64)
+                nc.vector.quantize_mx(
+                    out=g_codes[:].bitcast(E5M2_X4),
+                    scales=g_scales[:],
+                    in_=g_grouped[:].rearrange("p n j -> p (n j)"),
+                )
+                for i in range(GROUPS):
+                    group = slice(i * P, (i + 1) * P)
+                    bank = banks.tile([P, PASS_TOKENS], F32)
+                    nc.tensor.matmul_mx(
+                        out=bank[:],
+                        lhsT=k_codes[:, group].bitcast(E4M3_X4),
+                        lhsT_scale=k_scales[:, group],
+                        rhs=g_codes[:].bitcast(E5M2_X4),
+                        rhs_scale=g_scales[:],
+                        start=True,
+                        stop=True,
+                    )
+                    nc.scalar.copy(
+                        out=result[:, i, :, t * PASS_A : (t + 1) * PASS_A],
+                        in_=bank[:].rearrange("p (a d) -> p d a", a=PASS_A),
+                    )
+            nc.sync.dma_start(
+                out=out[b].rearrange("(m i) d a -> m (i d a)", i=GROUPS),
+                in_=result[:].rearrange("m i d a -> m (i d a)"),
+            )

@@ -90,10 +90,12 @@ def tile_sparseconv2d_t_kernel(tc, inputs, kernel, grad_out, out):
                         start=True,
                         stop=True,
                     )
-                    nc.scalar.copy(
-                        out=result[:, i, :, t * PASS_A : (t + 1) * PASS_A],
-                        in_=bank[:].rearrange("p (a d) -> p d a", a=PASS_A),
-                    )
+                    swapped = bank[:].rearrange("p (a d) -> p d a", a=PASS_A)
+                    place = result[:, i, :, t * PASS_A : (t + 1) * PASS_A]
+                    if i < GROUPS - 1:
+                        nc.scalar.copy(out=place, in_=swapped)
+                    else:
+                        nc.vector.tensor_copy(out=place, in_=swapped)
             nc.sync.dma_start(
                 out=out[b].rearrange("(m i) d a -> m (i d a)", i=GROUPS),
                 in_=result[:].rearrange("m i d a -> m (i d a)"),

@@ -90,13 +90,11 @@ def tile_sparseconv2d_t_kernel(tc, inputs, kernel, grad_out, out):
                         start=True,
                         stop=True,
                     )
-                    swapped = bank[:].rearrange("p (a d) -> p d a", a=PASS_A)
-                    place = result[:, i, :, t * PASS_A : (t + 1) * PASS_A]
-                    if i < GROUPS - 1:
-                        nc.scalar.copy(out=place, in_=swapped)
-                    else:
-                        nc.vector.tensor_copy(out=place, in_=swapped)
-            nc.sync.dma_start(
+                    nc.scalar.copy(
+                        out=result[:, i, :, t * PASS_A : (t + 1) * PASS_A],
+                        in_=bank[:].rearrange("p (a d) -> p d a", a=PASS_A),
+                    )
+            nc.scalar.dma_start(
                 out=out[b].rearrange("(m i) d a -> m (i d a)", i=GROUPS),
                 in_=result[:].rearrange("m i d a -> m (i d a)"),
             )

@@ -25,6 +25,7 @@ PASS_TOKENS = 512
 PASS_A = PASS_TOKENS // SIDE
 PASSES = TOKENS // PASS_TOKENS
 PSUM_BANKS = 8
+DMA_ALIGN = 256
 RUN = 4
 
 FLOPS = 2 * BATCH * TOKENS * FEATURES * CHANNELS
@@ -40,11 +41,11 @@ def tile_sparseconv2d_t_kernel(tc, inputs, kernel, grad_out, out):
         stage = ctx.enter_context(tc.tile_pool(name="stage", bufs=3))
         banks = ctx.enter_context(tc.psum_pool(name="banks", bufs=PSUM_BANKS))
 
-        k_rows = weights.tile([P, PACK, CHANNELS], BF16)
+        k_rows = weights.tile([P, PACK, CHANNELS], BF16, align_bytes=DMA_ALIGN)
         nc.sync.dma_start(out=k_rows[:], in_=kernel.rearrange("(p j) c -> p j c", j=PACK))
         g_rows = []
         for b in range(BATCH):
-            rows = loaded.tile([P, PACK, TOKENS], BF16, name="rows")
+            rows = loaded.tile([P, PACK, TOKENS], BF16, name="rows", align_bytes=DMA_ALIGN)
             nc.sync.dma_start(
                 out=rows[:], in_=grad_out[b].rearrange("(p j) a d -> p j (a d)", j=PACK)
             )
@@ -63,7 +64,7 @@ def tile_sparseconv2d_t_kernel(tc, inputs, kernel, grad_out, out):
         )
 
         for b in range(BATCH):
-            result = results.tile([P, GROUPS, SIDE, SIDE], F32)
+            result = results.tile([P, GROUPS, SIDE, SIDE], F32, align_bytes=DMA_ALIGN)
             for t in range(PASSES):
                 tokens = slice(t * PASS_TOKENS, (t + 1) * PASS_TOKENS)
                 g_grouped = stage.tile([P, PASS_TOKENS, PACK], BF16, align_bytes=64)

@@ -25,6 +25,8 @@ PASS_TOKENS = 512
 PASS_A = PASS_TOKENS // SIDE
 PASSES = TOKENS // PASS_TOKENS
 PSUM_BANKS = 8
+LOAD_RUNS = (1, 1, 2, 4)
+STORE_RUNS = (2, 2, 2, 1, 1)
 DMA_ALIGN = 256
 RUN = 4
 
@@ -36,20 +38,25 @@ def tile_sparseconv2d_t_kernel(tc, inputs, kernel, grad_out, out):
     nc = tc.nc
     with ExitStack() as ctx:
         weights = ctx.enter_context(tc.tile_pool(name="weights", bufs=1))
-        loaded = ctx.enter_context(tc.tile_pool(name="loaded", bufs=BATCH))
-        results = ctx.enter_context(tc.tile_pool(name="results", bufs=BATCH))
+        loaded = ctx.enter_context(tc.tile_pool(name="loaded", bufs=1))
+        results = ctx.enter_context(tc.tile_pool(name="results", bufs=1))
         stage = ctx.enter_context(tc.tile_pool(name="stage", bufs=3))
         banks = ctx.enter_context(tc.psum_pool(name="banks", bufs=PSUM_BANKS))
 
         k_rows = weights.tile([P, PACK, CHANNELS], BF16, align_bytes=DMA_ALIGN)
         nc.sync.dma_start(out=k_rows[:], in_=kernel.rearrange("(p j) c -> p j c", j=PACK))
         g_rows = []
-        for b in range(BATCH):
-            rows = loaded.tile([P, PACK, TOKENS], BF16, name="rows", align_bytes=DMA_ALIGN)
-            nc.sync.dma_start(
-                out=rows[:], in_=grad_out[b].rearrange("(p j) a d -> p j (a d)", j=PACK)
+        first = 0
+        for n in LOAD_RUNS:
+            rows = loaded.tile(
+                [P, n, PACK, TOKENS], BF16, name="rows%d" % first, align_bytes=DMA_ALIGN
             )
-            g_rows.append(rows)
+            nc.sync.dma_start(
+                out=rows[:].rearrange("p b j t -> p b (j t)"),
+                in_=grad_out[first : first + n].rearrange("b (p j) a d -> p b (j a d)", j=PACK),
+            )
+            g_rows.extend((rows, place) for place in range(n))
+            first += n
 
         k_grouped = weights.tile([P, GROUPS, P, PACK], BF16, align_bytes=64)
         nc.vector.tensor_copy(
@@ -63,39 +70,45 @@ def tile_sparseconv2d_t_kernel(tc, inputs, kernel, grad_out, out):
             in_=k_grouped[:].rearrange("p i m j -> p (i m j)"),
         )
 
-        for b in range(BATCH):
-            result = results.tile([P, GROUPS, SIDE, SIDE], F32, align_bytes=DMA_ALIGN)
-            for t in range(PASSES):
-                tokens = slice(t * PASS_TOKENS, (t + 1) * PASS_TOKENS)
-                g_grouped = stage.tile([P, PASS_TOKENS, PACK], BF16, align_bytes=64)
-                nc.vector.tensor_copy(
-                    out=g_grouped[:].rearrange("p (n r) j -> p n j r", r=RUN),
-                    in_=g_rows[b][:, :, tokens].rearrange("p j (n r) -> p n j r", r=RUN),
-                )
-                g_codes = stage.tile([P, PASS_TOKENS], U32, align_bytes=64)
-                g_scales = stage.tile([P, PASS_TOKENS], U8, align_bytes=64)
-                nc.vector.quantize_mx(
-                    out=g_codes[:].bitcast(E5M2_X4),
-                    scales=g_scales[:],
-                    in_=g_grouped[:].rearrange("p n j -> p (n j)"),
-                )
-                for i in range(GROUPS):
-                    group = slice(i * P, (i + 1) * P)
-                    bank = banks.tile([P, PASS_TOKENS], F32)
-                    nc.tensor.matmul_mx(
-                        out=bank[:],
-                        lhsT=k_codes[:, group].bitcast(E4M3_X4),
-                        lhsT_scale=k_scales[:, group],
-                        rhs=g_codes[:].bitcast(E5M2_X4),
-                        rhs_scale=g_scales[:],
-                        start=True,
-                        stop=True,
-                    )
-                    nc.scalar.copy(
-                        out=result[:, i, :, t * PASS_A : (t + 1) * PASS_A],
-                        in_=bank[:].rearrange("p (a d) -> p d a", a=PASS_A),
-                    )
-            nc.scalar.dma_start(
-                out=out[b].rearrange("(m i) d a -> m (i d a)", i=GROUPS),
-                in_=result[:].rearrange("m i d a -> m (i d a)"),
+        first = 0
+        for n in STORE_RUNS:
+            result = results.tile(
+                [P, n, GROUPS, SIDE, SIDE], F32, name="result%d" % first, align_bytes=DMA_ALIGN
             )
+            for place in range(n):
+                rows, row_place = g_rows[first + place]
+                for t in range(PASSES):
+                    tokens = slice(t * PASS_TOKENS, (t + 1) * PASS_TOKENS)
+                    g_grouped = stage.tile([P, PASS_TOKENS, PACK], BF16, align_bytes=64)
+                    nc.vector.tensor_copy(
+                        out=g_grouped[:].rearrange("p (n r) j -> p n j r", r=RUN),
+                        in_=rows[:, row_place, :, tokens].rearrange("p j (n r) -> p n j r", r=RUN),
+                    )
+                    g_codes = stage.tile([P, PASS_TOKENS], U32, align_bytes=64)
+                    g_scales = stage.tile([P, PASS_TOKENS], U8, align_bytes=64)
+                    nc.vector.quantize_mx(
+                        out=g_codes[:].bitcast(E5M2_X4),
+                        scales=g_scales[:],
+                        in_=g_grouped[:].rearrange("p n j -> p (n j)"),
+                    )
+                    for i in range(GROUPS):
+                        group = slice(i * P, (i + 1) * P)
+                        bank = banks.tile([P, PASS_TOKENS], F32)
+                        nc.tensor.matmul_mx(
+                            out=bank[:],
+                            lhsT=k_codes[:, group].bitcast(E4M3_X4),
+                            lhsT_scale=k_scales[:, group],
+                            rhs=g_codes[:].bitcast(E5M2_X4),
+                            rhs_scale=g_scales[:],
+                            start=True,
+                            stop=True,
+                        )
+                        nc.scalar.copy(
+                            out=result[:, place, i, :, t * PASS_A : (t + 1) * PASS_A],
+                            in_=bank[:].rearrange("p (a d) -> p d a", a=PASS_A),
+                        )
+            nc.scalar.dma_start(
+                out=out[first : first + n].rearrange("b (m i) d a -> m b (i d a)", i=GROUPS),
+                in_=result[:].rearrange("m b i d a -> m b (i d a)"),
+            )
+            first += n

@@ -27,7 +27,7 @@ PASSES = TOKENS // PASS_TOKENS
 PSUM_BANKS = 8
 LOAD_RUNS = (1, 1, 2, 4)
 STORE_RUNS = (2, 2, 2, 1, 1)
-DMA_ALIGN = 256
+DMA_ALIGN = 4096
 RUN = 4
 
 FLOPS = 2 * BATCH * TOKENS * FEATURES * CHANNELS
@@ -45,17 +45,13 @@ def tile_sparseconv2d_t_kernel(tc, inputs, kernel, grad_out, out):
 
         k_rows = weights.tile([P, PACK, CHANNELS], BF16, align_bytes=DMA_ALIGN)
         nc.sync.dma_start(out=k_rows[:], in_=kernel.rearrange("(p j) c -> p j c", j=PACK))
-        g_rows = []
+        rows = loaded.tile([P, BATCH, PACK, TOKENS], BF16, align_bytes=DMA_ALIGN)
         first = 0
         for n in LOAD_RUNS:
-            rows = loaded.tile(
-                [P, n, PACK, TOKENS], BF16, name="rows%d" % first, align_bytes=DMA_ALIGN
-            )
             nc.sync.dma_start(
-                out=rows[:].rearrange("p b j t -> p b (j t)"),
+                out=rows[:, first : first + n, :, :].rearrange("p b j t -> p b (j t)"),
                 in_=grad_out[first : first + n].rearrange("b (p j) a d -> p b (j a d)", j=PACK),
             )
-            g_rows.extend((rows, place) for place in range(n))
             first += n
 
         k_grouped = weights.tile([P, GROUPS, P, PACK], BF16, align_bytes=64)
@@ -70,19 +66,18 @@ def tile_sparseconv2d_t_kernel(tc, inputs, kernel, grad_out, out):
             in_=k_grouped[:].rearrange("p i m j -> p (i m j)"),
         )
 
+        result = results.tile(
+            [P, BATCH, GROUPS, SIDE, SIDE], F32, align_bytes=DMA_ALIGN
+        )
         first = 0
         for n in STORE_RUNS:
-            result = results.tile(
-                [P, n, GROUPS, SIDE, SIDE], F32, name="result%d" % first, align_bytes=DMA_ALIGN
-            )
-            for place in range(n):
-                rows, row_place = g_rows[first + place]
+            for b in range(first, first + n):
                 for t in range(PASSES):
                     tokens = slice(t * PASS_TOKENS, (t + 1) * PASS_TOKENS)
                     g_grouped = stage.tile([P, PASS_TOKENS, PACK], BF16, align_bytes=64)
                     nc.vector.tensor_copy(
                         out=g_grouped[:].rearrange("p (n r) j -> p n j r", r=RUN),
-                        in_=rows[:, row_place, :, tokens].rearrange("p j (n r) -> p n j r", r=RUN),
+                        in_=rows[:, b, :, tokens].rearrange("p j (n r) -> p n j r", r=RUN),
                     )
                     g_codes = stage.tile([P, PASS_TOKENS], U32, align_bytes=64)
                     g_scales = stage.tile([P, PASS_TOKENS], U8, align_bytes=64)
@@ -104,11 +99,11 @@ def tile_sparseconv2d_t_kernel(tc, inputs, kernel, grad_out, out):
                             stop=True,
                         )
                         nc.scalar.copy(
-                            out=result[:, place, i, :, t * PASS_A : (t + 1) * PASS_A],
+                            out=result[:, b, i, :, t * PASS_A : (t + 1) * PASS_A],
                             in_=bank[:].rearrange("p (a d) -> p d a", a=PASS_A),
                         )
             nc.scalar.dma_start(
                 out=out[first : first + n].rearrange("b (m i) d a -> m b (i d a)", i=GROUPS),
-                in_=result[:].rearrange("m b i d a -> m b (i d a)"),
+                in_=result[:, first : first + n, :, :, :].rearrange("m b i d a -> m b (i d a)"),
             )
             first += n

from contextlib import ExitStack

import concourse.mybir as mybir

BF16 = mybir.dt.bfloat16
F32 = mybir.dt.float32
U32 = mybir.dt.uint32
U8 = mybir.dt.uint8
E4M3_X4 = mybir.dt.float8_e4m3fn_x4
E5M2_X4 = mybir.dt.float8_e5m2_x4

P = 128
PACK = 4

BATCH = 8
FEATURES = 512
CHANNELS = 512
SIDE = 32
TOKENS = SIDE * SIDE

assert FEATURES == P * PACK

GROUPS = CHANNELS // P
PASS_TOKENS = 512
PASS_A = PASS_TOKENS // SIDE
PASSES = TOKENS // PASS_TOKENS
PSUM_BANKS = 8
LOAD_RUNS = (1, 1, 2, 4)
STORE_RUNS = (2, 2, 2, 1, 1)
DMA_ALIGN = 4096
RUN = 4

FLOPS = 2 * BATCH * TOKENS * FEATURES * CHANNELS
BYTES = 2 * BATCH * FEATURES * TOKENS + 2 * FEATURES * CHANNELS + 4 * BATCH * CHANNELS * TOKENS


def tile_sparseconv2d_t_kernel(tc, inputs, kernel, grad_out, out):
    nc = tc.nc
    with ExitStack() as ctx:
        weights = ctx.enter_context(tc.tile_pool(name="weights", bufs=1))
        loaded = ctx.enter_context(tc.tile_pool(name="loaded", bufs=1))
        results = ctx.enter_context(tc.tile_pool(name="results", bufs=1))
        stage = ctx.enter_context(tc.tile_pool(name="stage", bufs=3))
        banks = ctx.enter_context(tc.psum_pool(name="banks", bufs=PSUM_BANKS))

        k_rows = weights.tile([P, PACK, CHANNELS], BF16, align_bytes=DMA_ALIGN)
        nc.sync.dma_start(out=k_rows[:], in_=kernel.rearrange("(p j) c -> p j c", j=PACK))
        rows = loaded.tile([P, BATCH, PACK, TOKENS], BF16, align_bytes=DMA_ALIGN)
        first = 0
        for n in LOAD_RUNS:
            nc.sync.dma_start(
                out=rows[:, first : first + n, :, :].rearrange("p b j t -> p b (j t)"),
                in_=grad_out[first : first + n].rearrange("b (p j) a d -> p b (j a d)", j=PACK),
            )
            first += n

        k_grouped = weights.tile([P, GROUPS, P, PACK], BF16, align_bytes=64)
        nc.vector.tensor_copy(
            out=k_grouped[:], in_=k_rows[:].rearrange("p j (m i) -> p i m j", i=GROUPS)
        )
        k_codes = weights.tile([P, GROUPS * P], U32, align_bytes=64)
        k_scales = weights.tile([P, GROUPS * P], U8, align_bytes=64)
        nc.vector.quantize_mx(
            out=k_codes[:].bitcast(E4M3_X4),
            scales=k_scales[:],
            in_=k_grouped[:].rearrange("p i m j -> p (i m j)"),
        )

        result = results.tile(
            [P, BATCH, GROUPS, SIDE, SIDE], F32, align_bytes=DMA_ALIGN
        )
        first = 0
        for n in STORE_RUNS:
            for b in range(first, first + n):
                for t in range(PASSES):
                    tokens = slice(t * PASS_TOKENS, (t + 1) * PASS_TOKENS)
                    g_grouped = stage.tile([P, PASS_TOKENS, PACK], BF16, align_bytes=64)
                    nc.vector.tensor_copy(
                        out=g_grouped[:].rearrange("p (n r) j -> p n j r", r=RUN),
                        in_=rows[:, b, :, tokens].rearrange("p j (n r) -> p n j r", r=RUN),
                    )
                    g_codes = stage.tile([P, PASS_TOKENS], U32, align_bytes=64)
                    g_scales = stage.tile([P, PASS_TOKENS], U8, align_bytes=64)
                    nc.vector.quantize_mx(
                        out=g_codes[:].bitcast(E5M2_X4),
                        scales=g_scales[:],
                        in_=g_grouped[:].rearrange("p n j -> p (n j)"),
                    )
                    for i in range(GROUPS):
                        group = slice(i * P, (i + 1) * P)
                        bank = banks.tile([P, PASS_TOKENS], F32)
                        nc.tensor.matmul_mx(
                            out=bank[:],
                            lhsT=k_codes[:, group].bitcast(E4M3_X4),
                            lhsT_scale=k_scales[:, group],
                            rhs=g_codes[:].bitcast(E5M2_X4),
                            rhs_scale=g_scales[:],
                            start=True,
                            stop=True,
                        )
                        nc.scalar.copy(
                            out=result[:, b, i, :, t * PASS_A : (t + 1) * PASS_A],
                            in_=bank[:].rearrange("p (a d) -> p d a", a=PASS_A),
                        )
            nc.scalar.dma_start(
                out=out[first : first + n].rearrange("b (m i) d a -> m b (i d a)", i=GROUPS),
                in_=result[:, first : first + n, :, :, :].rearrange("m b i d a -> m b (i d a)"),
            )
            first += n
